import numpy as np
import ml_dtypes


def mxq(x, axis, fmt="e4m3"):
    dtype, down = {"e4m3": (ml_dtypes.float8_e4m3fn, 7), "e5m2": (ml_dtypes.float8_e5m2, 14)}[fmt]
    v = np.moveaxis(np.asarray(x, np.float32).astype(ml_dtypes.bfloat16).astype(np.float64), axis, -1)
    blocks = v.reshape(v.shape[:-1] + (-1, 32))
    amax = np.abs(blocks).max(-1, keepdims=True)
    byte = np.maximum(np.where(amax > 0, np.frexp(amax)[1] - 1 + 127, 0) - down, 1)
    scale = np.exp2(byte - 127.0)
    codes = (blocks / scale).astype(np.float32).astype(dtype).astype(np.float64)
    return np.moveaxis((codes * scale).reshape(v.shape), -1, axis)


WIDE = False


def mx_kscale(k):
    if not WIDE:
        return np.ones(k)
    levels = np.array([20, -20, 10, -10, 0])
    a = np.random.permutation(np.resize(levels, k // 512 * 4)).reshape(k // 512, 4)
    idx = np.arange(k)
    return np.exp2(a[idx // 512, idx % 128 // 32])


BF16 = ml_dtypes.bfloat16


def bf(x):
    return np.asarray(x, np.float32).astype(BF16)


def f64(x):
    return np.asarray(x).astype(np.float64)


BATCH, SIZE_IN, SIZE_OUT, STEPS = 512, 2048, 2048, 8


def _build_mask(size_in, size_out, steps):
    inp_el_counts = size_in // steps
    rows = np.arange(size_out)
    count = rows % inp_el_counts
    cols = np.arange(steps)[None, :] * inp_el_counts + count[:, None]
    mask = np.zeros((size_out, size_in))
    mask[rows[:, None], cols] = 1.0
    return mask


def setup_inputs():
    s = mx_kscale(BATCH)[:, None]
    bound = np.sqrt(3.0 / STEPS)
    x = np.random.standard_normal((BATCH, SIZE_IN)) * s
    weights = np.random.uniform(-bound, bound, (SIZE_OUT, SIZE_IN))
    bias = np.random.uniform(-0.5, 0.5, SIZE_OUT)
    mask = _build_mask(SIZE_IN, SIZE_OUT, STEPS)
    g = np.random.standard_normal((BATCH, SIZE_OUT)) * np.exp2(np.random.randint(-12, 1, (BATCH, 1))) / s
    return {"x": bf(x), "weights": bf(weights), "bias": bf(bias), "mask": bf(mask), "grad_out": bf(g)}


def reference(x, weights, bias, mask, grad_out):
    p = mxq(f64(grad_out), 0, "e5m2").T @ mxq(f64(x), 0, "e4m3")
    return p * f64(mask)

@@ -1,0 +1,103 @@
+from contextlib import ExitStack
+
+import concourse.mybir as mybir
+
+BF16 = mybir.dt.bfloat16
+F32 = mybir.dt.float32
+U32 = mybir.dt.uint32
+U8 = mybir.dt.uint8
+E4M3X4 = mybir.dt.float8_e4m3fn_x4
+E5M2X4 = mybir.dt.float8_e5m2_x4
+
+P = 128
+PACK = 4
+TOKENS = P * PACK
+SIZE_OUT = 2048
+SIZE_IN = 2048
+BANK = 512
+GROUPS = 4
+ROWS = 4
+CHUNK = P * ROWS
+N_BANKS = SIZE_IN // BANK
+STAGE_ROWS = 2
+
+FLOPS = 2 * TOKENS * SIZE_OUT * SIZE_IN
+BYTES = 2 * TOKENS * SIZE_OUT + 2 * TOKENS * SIZE_IN + 2 * SIZE_OUT * SIZE_IN + 4 * SIZE_OUT * SIZE_IN
+
+
+def tile_sparselayer_kernel(tc, x, weights, bias, mask, grad_out, out):
+    nc = tc.nc
+    mask_v = mask.rearrange("(b m e) i -> b m e i", b=GROUPS, m=P, e=ROWS)
+    out_v = out.rearrange("(b m e) i -> b m e i", b=GROUPS, m=P, e=ROWS)
+
+    with ExitStack() as ctx:
+        raw = ctx.enter_context(tc.tile_pool(name="raw", bufs=1))
+        keep = ctx.enter_context(tc.tile_pool(name="keep", bufs=1))
+        ring = ctx.enter_context(tc.tile_pool(name="ring", bufs=4))
+        stage = ctx.enter_context(tc.tile_pool(name="stage", bufs=6))
+        psum = ctx.enter_context(tc.psum_pool(name="psum", bufs=8))
+
+        g_raw = raw.tile([P, PACK, SIZE_OUT], BF16, name="g_raw")
+        x_raw = raw.tile([P, PACK, SIZE_IN], BF16, name="x_raw")
+        nc.sync.dma_start(out=g_raw[:], in_=grad_out.rearrange("(p t) o -> p t o", t=PACK))
+        nc.sync.dma_start(out=x_raw[:], in_=x.rearrange("(p t) i -> p t i", t=PACK))
+        mask_tiles = []
+        for b in range(GROUPS):
+            mk = keep.tile([P, ROWS, SIZE_IN], BF16, name="mask%d" % b)
+            nc.sync.dma_start(out=mk[:], in_=mask_v[b])
+            mask_tiles.append(mk)
+
+        def regroup(copy_fn, src, pattern):
+            grouped = ring.tile([P, CHUNK * PACK], BF16, name="grouped", align_bytes=64)
+            copy_fn(
+                out=grouped[:].rearrange(pattern, c=P, i=ROWS, t=PACK),
+                in_=src.rearrange("p t (c i) -> p c t i", i=ROWS),
+            )
+            return grouped
+
+        def quantise(grouped, fmt, label):
+            codes = keep.tile([P, CHUNK], U32, name="codes_" + label, align_bytes=64)
+            scales = keep.tile([P, CHUNK], U8, name="scales_" + label, align_bytes=64)
+            nc.vector.quantize_mx(out=codes[:].bitcast(fmt), scales=scales[:], in_=grouped[:])
+            return codes, scales
+
+        copies = [nc.vector.tensor_copy, nc.vector.tensor_copy, nc.scalar.copy, nc.scalar.copy]
+
+        g_grouped = [
+            regroup(copies[b], g_raw[:, :, b * CHUNK : (b + 1) * CHUNK], "p (i c t) -> p c t i")
+            for b in range(GROUPS)
+        ]
+        g_q = [quantise(g_grouped[b], E5M2X4, "g%d" % b) for b in range(GROUPS)]
+        x_grouped = [
+            regroup(copies[n], x_raw[:, :, n * CHUNK : (n + 1) * CHUNK], "p (c i t) -> p c t i")
+            for n in range(N_BANKS)
+        ]
+        x_q = [quantise(x_grouped[n], E4M3X4, "x%d" % n) for n in range(N_BANKS)]
+
+        for b in range(GROUPS):
+            g_codes, g_scales = g_q[b]
+            for e0 in range(0, ROWS, STAGE_ROWS):
+                staged = stage.tile([P, STAGE_ROWS, SIZE_IN], F32, name="staged")
+                for h in range(STAGE_ROWS):
+                    e = e0 + h
+                    rows = slice(e * P, (e + 1) * P)
+                    for n in range(N_BANKS):
+                        x_codes, x_scales = x_q[n]
+                        cols = slice(n * BANK, (n + 1) * BANK)
+                        acc = psum.tile([P, BANK], F32, name="acc")
+                        nc.tensor.matmul_mx(
+                            out=acc[:],
+                            lhsT=g_codes[:, rows].bitcast(E5M2X4),
+                            lhsT_scale=g_scales[:, rows],
+                            rhs=x_codes[:].bitcast(E4M3X4),
+                            rhs_scale=x_scales[:],
+                            start=True,
+                            stop=True,
+                        )
+                        nc.vector.tensor_tensor(
+                            out=staged[:, h, cols],
+                            in0=acc[:],
+                            in1=mask_tiles[b][:, e, cols],
+                            op=mybir.AluOpType.mult,
+                        )
+                nc.sync.dma_start(out=out_v[b][:, e0 : e0 + STAGE_ROWS, :], in_=staged[:])

@@ -19,7 +19,7 @@ GROUPS = 4
 ROWS = 4
 CHUNK = P * ROWS
 N_BANKS = SIZE_IN // BANK
-STAGE_ROWS = 2
+STORE_ROWS = [[4], [4], [4], [2, 2]]
 
 FLOPS = 2 * TOKENS * SIZE_OUT * SIZE_IN
 BYTES = 2 * TOKENS * SIZE_OUT + 2 * TOKENS * SIZE_IN + 2 * SIZE_OUT * SIZE_IN + 4 * SIZE_OUT * SIZE_IN
@@ -34,7 +34,7 @@ def tile_sparselayer_kernel(tc, x, weights, bias, mask, grad_out, out):
         raw = ctx.enter_context(tc.tile_pool(name="raw", bufs=1))
         keep = ctx.enter_context(tc.tile_pool(name="keep", bufs=1))
         ring = ctx.enter_context(tc.tile_pool(name="ring", bufs=4))
-        stage = ctx.enter_context(tc.tile_pool(name="stage", bufs=6))
+        stage = ctx.enter_context(tc.tile_pool(name="stage", bufs=3))
         psum = ctx.enter_context(tc.psum_pool(name="psum", bufs=8))
 
         g_raw = raw.tile([P, PACK, SIZE_OUT], BF16, name="g_raw")
@@ -76,9 +76,10 @@ def tile_sparselayer_kernel(tc, x, weights, bias, mask, grad_out, out):
 
         for b in range(GROUPS):
             g_codes, g_scales = g_q[b]
-            for e0 in range(0, ROWS, STAGE_ROWS):
-                staged = stage.tile([P, STAGE_ROWS, SIZE_IN], F32, name="staged")
-                for h in range(STAGE_ROWS):
+            e0 = 0
+            for count in STORE_ROWS[b]:
+                staged = stage.tile([P, ROWS, SIZE_IN], F32, name="staged")
+                for h in range(count):
                     e = e0 + h
                     rows = slice(e * P, (e + 1) * P)
                     for n in range(N_BANKS):
@@ -100,4 +101,5 @@ def tile_sparselayer_kernel(tc, x, weights, bias, mask, grad_out, out):
                             in1=mask_tiles[b][:, e, cols],
                             op=mybir.AluOpType.mult,
                         )
-                nc.sync.dma_start(out=out_v[b][:, e0 : e0 + STAGE_ROWS, :], in_=staged[:])
+                nc.sync.dma_start(out=out_v[b][:, e0 : e0 + count, :], in_=staged[:, 0:count, :])
+                e0 += count

@@ -39,8 +39,8 @@ def tile_sparselayer_kernel(tc, x, weights, bias, mask, grad_out, out):
 
         g_raw = raw.tile([P, PACK, SIZE_OUT], BF16, name="g_raw")
         x_raw = raw.tile([P, PACK, SIZE_IN], BF16, name="x_raw")
-        nc.sync.dma_start(out=g_raw[:], in_=grad_out.rearrange("(p t) o -> p t o", t=PACK))
         nc.sync.dma_start(out=x_raw[:], in_=x.rearrange("(p t) i -> p t i", t=PACK))
+        nc.sync.dma_start(out=g_raw[:], in_=grad_out.rearrange("(p t) o -> p t o", t=PACK))
         mask_tiles = []
         for b in range(GROUPS):
             mk = keep.tile([P, ROWS, SIZE_IN], BF16, name="mask%d" % b)
@@ -55,24 +55,33 @@ def tile_sparselayer_kernel(tc, x, weights, bias, mask, grad_out, out):
             )
             return grouped
 
+        def regroup_g(copy_fn, b):
+            return regroup(copy_fn, g_raw[:, :, b * CHUNK : (b + 1) * CHUNK], "p (i c t) -> p c t i")
+
+        def regroup_x(copy_fn, n):
+            return regroup(copy_fn, x_raw[:, :, n * CHUNK : (n + 1) * CHUNK], "p (c i t) -> p c t i")
+
         def quantise(grouped, fmt, label):
             codes = keep.tile([P, CHUNK], U32, name="codes_" + label, align_bytes=64)
             scales = keep.tile([P, CHUNK], U8, name="scales_" + label, align_bytes=64)
             nc.vector.quantize_mx(out=codes[:].bitcast(fmt), scales=scales[:], in_=grouped[:])
             return codes, scales
 
-        copies = [nc.vector.tensor_copy, nc.vector.tensor_copy, nc.scalar.copy, nc.scalar.copy]
+        ctx.enter_context(tc.manual_schedule(engines={mybir.EngineType.DVE}))
 
-        g_grouped = [
-            regroup(copies[b], g_raw[:, :, b * CHUNK : (b + 1) * CHUNK], "p (i c t) -> p c t i")
-            for b in range(GROUPS)
+        x0_grouped = regroup_x(nc.vector.tensor_copy, 0)
+        x2_grouped = regroup_x(nc.scalar.copy, 2)
+        x1_grouped = regroup_x(nc.vector.tensor_copy, 1)
+        x3_grouped = regroup_x(nc.scalar.copy, 3)
+        x_q = [
+            quantise(x0_grouped, E4M3X4, "x0"),
+            quantise(x1_grouped, E4M3X4, "x1"),
+            quantise(x2_grouped, E4M3X4, "x2"),
+            quantise(x3_grouped, E4M3X4, "x3"),
         ]
-        g_q = [quantise(g_grouped[b], E5M2X4, "g%d" % b) for b in range(GROUPS)]
-        x_grouped = [
-            regroup(copies[n], x_raw[:, :, n * CHUNK : (n + 1) * CHUNK], "p (c i t) -> p c t i")
-            for n in range(N_BANKS)
-        ]
-        x_q = [quantise(x_grouped[n], E4M3X4, "x%d" % n) for n in range(N_BANKS)]
+        g0_grouped = regroup_g(nc.vector.tensor_copy, 0)
+        g_later = [regroup_g(nc.scalar.copy, b) for b in range(1, GROUPS)]
+        g_q = [quantise(g0_grouped, E5M2X4, "g0")]
 
         for b in range(GROUPS):
             g_codes, g_scales = g_q[b]
@@ -101,5 +110,7 @@ def tile_sparselayer_kernel(tc, x, weights, bias, mask, grad_out, out):
                             in1=mask_tiles[b][:, e, cols],
                             op=mybir.AluOpType.mult,
                         )
+                    if e == 1 and b + 1 < GROUPS:
+                        g_q.append(quantise(g_later[b], E5M2X4, "g%d" % (b + 1)))
                 nc.sync.dma_start(out=out_v[b][:, e0 : e0 + count, :], in_=staged[:, 0:count, :])
                 e0 += count

@@ -20,6 +20,7 @@ ROWS = 4
 CHUNK = P * ROWS
 N_BANKS = SIZE_IN // BANK
 STORE_ROWS = [[4], [4], [4], [2, 2]]
+DMA_ALIGN = 512
 
 FLOPS = 2 * TOKENS * SIZE_OUT * SIZE_IN
 BYTES = 2 * TOKENS * SIZE_OUT + 2 * TOKENS * SIZE_IN + 2 * SIZE_OUT * SIZE_IN + 4 * SIZE_OUT * SIZE_IN
@@ -37,13 +38,13 @@ def tile_sparselayer_kernel(tc, x, weights, bias, mask, grad_out, out):
         stage = ctx.enter_context(tc.tile_pool(name="stage", bufs=3))
         psum = ctx.enter_context(tc.psum_pool(name="psum", bufs=8))
 
-        g_raw = raw.tile([P, PACK, SIZE_OUT], BF16, name="g_raw")
-        x_raw = raw.tile([P, PACK, SIZE_IN], BF16, name="x_raw")
+        g_raw = raw.tile([P, PACK, SIZE_OUT], BF16, name="g_raw", align_bytes=DMA_ALIGN)
+        x_raw = raw.tile([P, PACK, SIZE_IN], BF16, name="x_raw", align_bytes=DMA_ALIGN)
         nc.sync.dma_start(out=x_raw[:], in_=x.rearrange("(p t) i -> p t i", t=PACK))
         nc.sync.dma_start(out=g_raw[:], in_=grad_out.rearrange("(p t) o -> p t o", t=PACK))
         mask_tiles = []
         for b in range(GROUPS):
-            mk = keep.tile([P, ROWS, SIZE_IN], BF16, name="mask%d" % b)
+            mk = keep.tile([P, ROWS, SIZE_IN], BF16, name="mask%d" % b, align_bytes=DMA_ALIGN)
             nc.sync.dma_start(out=mk[:], in_=mask_v[b])
             mask_tiles.append(mk)
 
@@ -87,7 +88,7 @@ def tile_sparselayer_kernel(tc, x, weights, bias, mask, grad_out, out):
             g_codes, g_scales = g_q[b]
             e0 = 0
             for count in STORE_ROWS[b]:
-                staged = stage.tile([P, ROWS, SIZE_IN], F32, name="staged")
+                staged = stage.tile([P, ROWS, SIZE_IN], F32, name="staged", align_bytes=DMA_ALIGN)
                 for h in range(count):
                     e = e0 + h
                     rows = slice(e * P, (e + 1) * P)

@@ -83,6 +83,9 @@ def tile_sparselayer_kernel(tc, x, weights, bias, mask, grad_out, out):
         g0_grouped = regroup_g(nc.vector.tensor_copy, 0)
         g_later = [regroup_g(nc.scalar.copy, b) for b in range(1, GROUPS)]
         g_q = [quantise(g0_grouped, E5M2X4, "g0")]
+        spare = weights.rearrange("(p r) i -> p r i", r=PACK)
+        nc.sync.dma_start(out=x_raw[64:96:4, :, :], in_=spare[0:8])
+        nc.sync.dma_start(out=x_raw[96:128:4, :, :], in_=spare[8:16])
 
         for b in range(GROUPS):
             g_codes, g_scales = g_q[b]

from contextlib import ExitStack

import concourse.mybir as mybir

BF16 = mybir.dt.bfloat16
F32 = mybir.dt.float32
U32 = mybir.dt.uint32
U8 = mybir.dt.uint8
E4M3X4 = mybir.dt.float8_e4m3fn_x4
E5M2X4 = mybir.dt.float8_e5m2_x4

P = 128
PACK = 4
TOKENS = P * PACK
SIZE_OUT = 2048
SIZE_IN = 2048
BANK = 512
GROUPS = 4
ROWS = 4
CHUNK = P * ROWS
N_BANKS = SIZE_IN // BANK
STORE_ROWS = [[4], [4], [4], [2, 2]]
DMA_ALIGN = 512

FLOPS = 2 * TOKENS * SIZE_OUT * SIZE_IN
BYTES = 2 * TOKENS * SIZE_OUT + 2 * TOKENS * SIZE_IN + 2 * SIZE_OUT * SIZE_IN + 4 * SIZE_OUT * SIZE_IN


def tile_sparselayer_kernel(tc, x, weights, bias, mask, grad_out, out):
    nc = tc.nc
    mask_v = mask.rearrange("(b m e) i -> b m e i", b=GROUPS, m=P, e=ROWS)
    out_v = out.rearrange("(b m e) i -> b m e i", b=GROUPS, m=P, e=ROWS)

    with ExitStack() as ctx:
        raw = ctx.enter_context(tc.tile_pool(name="raw", bufs=1))
        keep = ctx.enter_context(tc.tile_pool(name="keep", bufs=1))
        ring = ctx.enter_context(tc.tile_pool(name="ring", bufs=4))
        stage = ctx.enter_context(tc.tile_pool(name="stage", bufs=3))
        psum = ctx.enter_context(tc.psum_pool(name="psum", bufs=8))

        g_raw = raw.tile([P, PACK, SIZE_OUT], BF16, name="g_raw", align_bytes=DMA_ALIGN)
        x_raw = raw.tile([P, PACK, SIZE_IN], BF16, name="x_raw", align_bytes=DMA_ALIGN)
        nc.sync.dma_start(out=x_raw[:], in_=x.rearrange("(p t) i -> p t i", t=PACK))
        nc.sync.dma_start(out=g_raw[:], in_=grad_out.rearrange("(p t) o -> p t o", t=PACK))
        mask_tiles = []
        for b in range(GROUPS):
            mk = keep.tile([P, ROWS, SIZE_IN], BF16, name="mask%d" % b, align_bytes=DMA_ALIGN)
            nc.sync.dma_start(out=mk[:], in_=mask_v[b])
            mask_tiles.append(mk)

        def regroup(copy_fn, src, pattern):
            grouped = ring.tile([P, CHUNK * PACK], BF16, name="grouped", align_bytes=64)
            copy_fn(
                out=grouped[:].rearrange(pattern, c=P, i=ROWS, t=PACK),
                in_=src.rearrange("p t (c i) -> p c t i", i=ROWS),
            )
            return grouped

        def regroup_g(copy_fn, b):
            return regroup(copy_fn, g_raw[:, :, b * CHUNK : (b + 1) * CHUNK], "p (i c t) -> p c t i")

        def regroup_x(copy_fn, n):
            return regroup(copy_fn, x_raw[:, :, n * CHUNK : (n + 1) * CHUNK], "p (c i t) -> p c t i")

        def quantise(grouped, fmt, label):
            codes = keep.tile([P, CHUNK], U32, name="codes_" + label, align_bytes=64)
            scales = keep.tile([P, CHUNK], U8, name="scales_" + label, align_bytes=64)
            nc.vector.quantize_mx(out=codes[:].bitcast(fmt), scales=scales[:], in_=grouped[:])
            return codes, scales

        ctx.enter_context(tc.manual_schedule(engines={mybir.EngineType.DVE}))

        x0_grouped = regroup_x(nc.vector.tensor_copy, 0)
        x2_grouped = regroup_x(nc.scalar.copy, 2)
        x1_grouped = regroup_x(nc.vector.tensor_copy, 1)
        x3_grouped = regroup_x(nc.scalar.copy, 3)
        x_q = [
            quantise(x0_grouped, E4M3X4, "x0"),
            quantise(x1_grouped, E4M3X4, "x1"),
            quantise(x2_grouped, E4M3X4, "x2"),
            quantise(x3_grouped, E4M3X4, "x3"),
        ]
        g0_grouped = regroup_g(nc.vector.tensor_copy, 0)
        g_later = [regroup_g(nc.scalar.copy, b) for b in range(1, GROUPS)]
        g_q = [quantise(g0_grouped, E5M2X4, "g0")]
        spare = weights.rearrange("(p r) i -> p r i", r=PACK)
        nc.sync.dma_start(out=x_raw[64:96:4, :, :], in_=spare[0:8])
        nc.sync.dma_start(out=x_raw[96:128:4, :, :], in_=spare[8:16])

        for b in range(GROUPS):
            g_codes, g_scales = g_q[b]
            e0 = 0
            for count in STORE_ROWS[b]:
                staged = stage.tile([P, ROWS, SIZE_IN], F32, name="staged", align_bytes=DMA_ALIGN)
                for h in range(count):
                    e = e0 + h
                    rows = slice(e * P, (e + 1) * P)
                    for n in range(N_BANKS):
                        x_codes, x_scales = x_q[n]
                        cols = slice(n * BANK, (n + 1) * BANK)
                        acc = psum.tile([P, BANK], F32, name="acc")
                        nc.tensor.matmul_mx(
                            out=acc[:],
                            lhsT=g_codes[:, rows].bitcast(E5M2X4),
                            lhsT_scale=g_scales[:, rows],
                            rhs=x_codes[:].bitcast(E4M3X4),
                            rhs_scale=x_scales[:],
                            start=True,
                            stop=True,
                        )
                        nc.vector.tensor_tensor(
                            out=staged[:, h, cols],
                            in0=acc[:],
                            in1=mask_tiles[b][:, e, cols],
                            op=mybir.AluOpType.mult,
                        )
                    if e == 1 and b + 1 < GROUPS:
                        g_q.append(quantise(g_later[b], E5M2X4, "g%d" % (b + 1)))
                nc.sync.dma_start(out=out_v[b][:, e0 : e0 + count, :], in_=staged[:, 0:count, :])
                e0 += count
